import numpy as np
import ml_dtypes


def mxq(x, axis, fmt="e4m3"):
    dtype, down = {"e4m3": (ml_dtypes.float8_e4m3fn, 7), "e5m2": (ml_dtypes.float8_e5m2, 14)}[fmt]
    v = np.moveaxis(np.asarray(x, np.float32).astype(ml_dtypes.bfloat16).astype(np.float64), axis, -1)
    blocks = v.reshape(v.shape[:-1] + (-1, 32))
    amax = np.abs(blocks).max(-1, keepdims=True)
    byte = np.maximum(np.where(amax > 0, np.frexp(amax)[1] - 1 + 127, 0) - down, 1)
    scale = np.exp2(byte - 127.0)
    codes = (blocks / scale).astype(np.float32).astype(dtype).astype(np.float64)
    return np.moveaxis((codes * scale).reshape(v.shape), -1, axis)


WIDE = False


def mx_kscale(k):
    if not WIDE:
        return np.ones(k)
    levels = np.array([10, -10, 5, -5, 0])
    a = np.random.permutation(np.resize(levels, k // 512 * 4)).reshape(k // 512, 4)
    idx = np.arange(k)
    return np.exp2(a[idx // 512, idx % 128 // 32])


BF16 = ml_dtypes.bfloat16


def bf(x):
    return np.asarray(x, np.float32).astype(BF16)


def f64(x):
    return np.asarray(x).astype(np.float64)


BS, DC, R, C = 8, 128, 32, 32
N = R * C
THRESH = 0.85


def setup_inputs():
    s = mx_kscale(N)
    u = s / s.min()
    g = 2.0 ** np.round(np.log2(u.mean()))
    seg = np.random.standard_normal((BS, DC, R, C)) * 0.1 * np.sqrt(N)
    W0 = f64(bf(np.random.random_sample((BS, N, N))))
    return {"seg": bf(seg * (g / u).reshape(1, 1, R, C)),
            "W": bf(np.where(W0 > THRESH, W0 * u, W0))}


def reference(seg, W):
    seg, W = f64(seg), f64(W)
    bs, d, r, c = seg.shape
    Wt = np.where(W > THRESH, W, 0.0)
    D = Wt / Wt.sum(axis=-1, keepdims=True)
    seg_flat = seg.reshape(bs, d, r * c)
    out = mxq(seg_flat, 2, "e4m3") @ mxq(D, 2, "e4m3").transpose(0, 2, 1)
    return out.reshape(bs, d, r, c)

@@ -1,0 +1,143 @@
+from contextlib import ExitStack
+
+import concourse.mybir as mybir
+from concourse.masks import make_identity
+
+BF16 = mybir.dt.bfloat16
+F32 = mybir.dt.float32
+U32 = mybir.dt.uint32
+U8 = mybir.dt.uint8
+FP8X4 = mybir.dt.float8_e4m3fn_x4
+ALU = mybir.AluOpType
+ACT = mybir.ActivationFunctionType
+
+BS = 8
+DC = 128
+N = 1024
+P = 128
+THRESH = 0.85
+FLOPS = 2 * BS * DC * N * N
+
+ROWS = 4
+UNITS = BS * 2
+SCALE_ON_SCALAR = (3,)
+
+
+def tile_regu_diff_t_kernel(tc, seg, W, out):
+    nc = tc.nc
+    seg_v = seg.rearrange("b d r c -> d b (r c)")
+    w_v = W.rearrange("b (c j p) n -> b c p j n", c=2, j=ROWS, p=P)
+    out_v = out.rearrange("b d r c -> b d (r c)")
+
+    with ExitStack() as ctx:
+        const = ctx.enter_context(tc.tile_pool(name="const", bufs=1))
+        wpool = ctx.enter_context(tc.tile_pool(name="wpool", bufs=5))
+        dpool = ctx.enter_context(tc.tile_pool(name="dpool", bufs=3))
+        small = ctx.enter_context(tc.tile_pool(name="small", bufs=4))
+        gpool = ctx.enter_context(tc.tile_pool(name="gpool", bufs=3))
+        qpool = ctx.enter_context(tc.tile_pool(name="qpool", bufs=3))
+        opool = ctx.enter_context(tc.tile_pool(name="opool", bufs=3))
+        tpsum = ctx.enter_context(tc.psum_pool(name="tpsum", bufs=5))
+        apsum = ctx.enter_context(tc.psum_pool(name="apsum", bufs=2))
+
+        ident = const.tile([P, P], BF16)
+        make_identity(nc, ident[:])
+
+        seg_sb = const.tile([P, BS, N], BF16)
+        seg_grouped = const.tile([P, BS, 2, DC, 4], BF16, align_bytes=64)
+        seg_codes = const.tile([P, BS, 2, DC], U32, align_bytes=64)
+        seg_scales = const.tile([P, BS, 2, DC], U8, align_bytes=64)
+
+        w_tiles = {}
+
+        def load_w(u, pieces):
+            b, c = divmod(u, 2)
+            w_sb = wpool.tile([P, ROWS, N], BF16, name="w_sb")
+            step = ROWS // pieces
+            for i in range(pieces):
+                nc.sync.dma_start(
+                    out=w_sb[:, i * step : (i + 1) * step, :],
+                    in_=w_v[b, c, :, i * step : (i + 1) * step, :],
+                )
+            w_tiles[u] = w_sb
+
+        def load_seg(lo, hi):
+            nc.sync.dma_start(out=seg_sb[:, lo:hi, :], in_=seg_v[:, lo:hi, :])
+
+        def transpose_rows(src):
+            bank = tpsum.tile([P, 8, P], BF16, name="bank")
+            for k in range(8):
+                nc.tensor.transpose(bank[:, k, :], src[:, k * P : (k + 1) * P], ident[:])
+            return bank[:].rearrange("p (g t) m -> p g m t", g=2)
+
+        load_w(0, 4)
+        load_seg(0, 4)
+        load_w(1, 2)
+        load_seg(4, 8)
+        for u in range(2, 5):
+            load_w(u, 1)
+
+        for b in range(BS):
+            nc.scalar.copy(out=seg_grouped[:, b], in_=transpose_rows(seg_sb[:, b, :]))
+        for h in range(2):
+            nc.vector.quantize_mx(
+                out=seg_codes[:, 4 * h : 4 * h + 4].rearrange("p b g d -> p (b g d)").bitcast(FP8X4),
+                scales=seg_scales[:, 4 * h : 4 * h + 4].rearrange("p b g d -> p (b g d)"),
+                in_=seg_grouped[:, 4 * h : 4 * h + 4].rearrange("p b g d t -> p (b g d t)"),
+            )
+
+        for u in range(UNITS):
+            b, c = divmod(u, 2)
+            if u + 5 < UNITS:
+                load_w(u + 5, 1)
+            w_sb = w_tiles.pop(u)
+            d_sb = dpool.tile([P, ROWS, N], BF16, name="d_sb")
+            sums = small.tile([P, ROWS], F32, name="sums")
+            rinv = small.tile([P, ROWS], F32, name="rinv")
+            for j in range(ROWS):
+                nc.vector.scalar_tensor_tensor(
+                    out=d_sb[:, j, :],
+                    in0=w_sb[:, j, :],
+                    scalar=THRESH,
+                    in1=w_sb[:, j, :],
+                    op0=ALU.is_gt,
+                    op1=ALU.mult,
+                    accum_out=sums[:, j : j + 1],
+                )
+            nc.vector.reciprocal(rinv[:], sums[:])
+            grouped = gpool.tile([P, 2, ROWS * P, 4], BF16, name="grouped", align_bytes=64)
+            for j in range(ROWS):
+                if j in SCALE_ON_SCALAR:
+                    nc.scalar.activation(
+                        out=d_sb[:, j, :], in_=d_sb[:, j, :], func=ACT.Copy, scale=rinv[:, j : j + 1]
+                    )
+                else:
+                    nc.vector.tensor_scalar_mul(
+                        out=d_sb[:, j, :], in0=d_sb[:, j, :], scalar1=rinv[:, j : j + 1]
+                    )
+            for j in range(ROWS):
+                nc.scalar.copy(
+                    out=grouped[:, :, j * P : (j + 1) * P, :], in_=transpose_rows(d_sb[:, j, :])
+                )
+            codes = qpool.tile([P, 2 * ROWS * P], U32, name="codes", align_bytes=64)
+            scales = qpool.tile([P, 2 * ROWS * P], U8, name="scales", align_bytes=64)
+            nc.vector.quantize_mx(
+                out=codes[:].bitcast(FP8X4),
+                scales=scales[:],
+                in_=grouped[:].rearrange("p g m t -> p (g m t)"),
+            )
+            acc = apsum.tile([P, ROWS * P], F32, name="acc")
+            for g in range(2):
+                cols = slice(g * ROWS * P, (g + 1) * ROWS * P)
+                nc.tensor.matmul_mx(
+                    out=acc[:],
+                    lhsT=seg_codes[:, b, g, :].bitcast(FP8X4),
+                    lhsT_scale=seg_scales[:, b, g, :],
+                    rhs=codes[:, cols].bitcast(FP8X4),
+                    rhs_scale=scales[:, cols],
+                    start=(g == 0),
+                    stop=(g == 1),
+                )
+            o_sb = opool.tile([P, ROWS * P], F32, name="o_sb")
+            nc.scalar.copy(out=o_sb[:], in_=acc[:])
+            nc.sync.dma_start(out=out_v[b][:, c * ROWS * P : (c + 1) * ROWS * P], in_=o_sb[:])

@@ -18,51 +18,120 @@ P = 128
 THRESH = 0.85
 FLOPS = 2 * BS * DC * N * N
 
-ROWS = 4
-UNITS = BS * 2
-SCALE_ON_SCALAR = (3,)
+def make_cfg():
+    return {
+        "prefetch": 6,
+        "seg_tick": [0, 1, 2, 3, 4, 5, 6, 7],
+        "lag_b": 2,
+        "lag_c": 1,
+        "lag_q": 2,
+        "lag_x": 1,
+        "b_on_act": set(r for r in range(56) if r % 4 == 3 or r % 12 == 1),
+        "c_on_dve": set([60, 62]),
+        "x_on_dve": set([]),
+    }
+
+
+GROUP_SIZES = [4] * 15 + [2, 2]
+
+
+def make_groups():
+    groups = []
+    first = 0
+    for size in GROUP_SIZES:
+        groups.append((first, size))
+        first += size
+    return groups
+
+
+def make_plan(cfg):
+    groups = make_groups()
+    n_rows = 64
+    group_of = {}
+    for g, (first, size) in enumerate(groups):
+        for i in range(size):
+            group_of[first + i] = g
+    at = {}
+
+    def put(tick, entry):
+        if tick not in at:
+            at[tick] = []
+        at[tick].append(entry)
+
+    order = []
+    for r in range(8):
+        order.append(("LW", (r, 1), "sync"))
+        order.append(("LS", r, "sync"))
+    for r in range(8, cfg["prefetch"] * 4, 4):
+        order.append(("LW", (r, 4), "sync"))
+    for r in range(cfg["prefetch"] * 4, n_rows, 4):
+        put(r - cfg["prefetch"] * 4 + 4, ("LW", (r, 4), "sync"))
+    for b in range(8):
+        t0 = cfg["seg_tick"][b]
+        put(t0, ("ST", b, "pe"))
+        put(t0 + 1, ("SC", b, "act"))
+        put(t0 + 3, ("SQ", b, "dve"))
+    for r in range(n_rows):
+        put(r, ("A", r, "dve"))
+    for g, (first, size) in enumerate(groups):
+        last = first + size - 1
+        put(last + 1, ("R", g, "dve"))
+        for i in range(size):
+            r = first + i
+            tb = last + cfg["lag_b"] + i
+            put(tb, ("B", r, "act" if r in cfg["b_on_act"] else "dve"))
+            put(tb, ("T", r, "pe"))
+            put(tb + cfg["lag_c"], ("C", r, "dve" if r in cfg["c_on_dve"] else "act"))
+        tq = last + cfg["lag_b"] + size - 1 + cfg["lag_c"] + cfg["lag_q"]
+        put(tq, ("Q", g, "dve"))
+        put(tq, ("M", g, "pe"))
+        put(tq + cfg["lag_x"], ("X", g, "dve" if g in cfg["x_on_dve"] else "act"))
+        put(tq + cfg["lag_x"], ("O", g, "sync"))
+    rank = {"LW": 0, "LS": 0, "A": 1, "R": 2, "SQ": 3, "B": 4, "ST": 5, "T": 5, "SC": 6, "C": 6, "Q": 7, "M": 8, "X": 9, "O": 10}
+    for tick in sorted(at):
+        order.extend(sorted(at[tick], key=lambda e: rank[e[0]]))
+    return order
 
 
 def tile_regu_diff_t_kernel(tc, seg, W, out):
     nc = tc.nc
-    seg_v = seg.rearrange("b d r c -> d b (r c)")
-    w_v = W.rearrange("b (c j p) n -> b c p j n", c=2, j=ROWS, p=P)
+    seg_v = seg.rearrange("b d r c -> b d (r c)")
+    w_v = W.rearrange("b (j p) n -> b p j n", p=P)
     out_v = out.rearrange("b d r c -> b d (r c)")
+    groups = make_groups()
+    group_of = {}
+    for g, (first, size) in enumerate(groups):
+        for i in range(size):
+            group_of[first + i] = g
 
     with ExitStack() as ctx:
         const = ctx.enter_context(tc.tile_pool(name="const", bufs=1))
-        wpool = ctx.enter_context(tc.tile_pool(name="wpool", bufs=5))
-        dpool = ctx.enter_context(tc.tile_pool(name="dpool", bufs=3))
-        small = ctx.enter_context(tc.tile_pool(name="small", bufs=4))
-        gpool = ctx.enter_context(tc.tile_pool(name="gpool", bufs=3))
+        wpool = ctx.enter_context(tc.tile_pool(name="wpool", bufs=make_cfg()["prefetch"]))
+        dpool = ctx.enter_context(tc.tile_pool(name="dpool", bufs=4))
+        small = ctx.enter_context(tc.tile_pool(name="small", bufs=6))
+        gpool = ctx.enter_context(tc.tile_pool(name="gpool", bufs=5))
         qpool = ctx.enter_context(tc.tile_pool(name="qpool", bufs=3))
         opool = ctx.enter_context(tc.tile_pool(name="opool", bufs=3))
-        tpsum = ctx.enter_context(tc.psum_pool(name="tpsum", bufs=5))
+        tpsum = ctx.enter_context(tc.psum_pool(name="tpsum", bufs=6))
         apsum = ctx.enter_context(tc.psum_pool(name="apsum", bufs=2))
 
         ident = const.tile([P, P], BF16)
         make_identity(nc, ident[:])
-
         seg_sb = const.tile([P, BS, N], BF16)
         seg_grouped = const.tile([P, BS, 2, DC, 4], BF16, align_bytes=64)
         seg_codes = const.tile([P, BS, 2, DC], U32, align_bytes=64)
         seg_scales = const.tile([P, BS, 2, DC], U8, align_bytes=64)
 
-        w_tiles = {}
-
-        def load_w(u, pieces):
-            b, c = divmod(u, 2)
-            w_sb = wpool.tile([P, ROWS, N], BF16, name="w_sb")
-            step = ROWS // pieces
-            for i in range(pieces):
-                nc.sync.dma_start(
-                    out=w_sb[:, i * step : (i + 1) * step, :],
-                    in_=w_v[b, c, :, i * step : (i + 1) * step, :],
-                )
-            w_tiles[u] = w_sb
-
-        def load_seg(lo, hi):
-            nc.sync.dma_start(out=seg_sb[:, lo:hi, :], in_=seg_v[:, lo:hi, :])
+        w_of = {}
+        d_of = {}
+        sums_of = {}
+        rinv_of = {}
+        bank_of = {}
+        seg_bank_of = {}
+        grouped_of = {}
+        codes_of = {}
+        acc_of = {}
+        o_of = {}
 
         def transpose_rows(src):
             bank = tpsum.tile([P, 8, P], BF16, name="bank")
@@ -70,74 +139,106 @@ def tile_regu_diff_t_kernel(tc, seg, W, out):
                 nc.tensor.transpose(bank[:, k, :], src[:, k * P : (k + 1) * P], ident[:])
             return bank[:].rearrange("p (g t) m -> p g m t", g=2)
 
-        load_w(0, 4)
-        load_seg(0, 4)
-        load_w(1, 2)
-        load_seg(4, 8)
-        for u in range(2, 5):
-            load_w(u, 1)
+        def copy_on(engine, dst, src):
+            if engine == "act":
+                nc.scalar.copy(out=dst, in_=src)
+            else:
+                nc.vector.tensor_copy(out=dst, in_=src)
 
-        for b in range(BS):
-            nc.scalar.copy(out=seg_grouped[:, b], in_=transpose_rows(seg_sb[:, b, :]))
-        for h in range(2):
-            nc.vector.quantize_mx(
-                out=seg_codes[:, 4 * h : 4 * h + 4].rearrange("p b g d -> p (b g d)").bitcast(FP8X4),
-                scales=seg_scales[:, 4 * h : 4 * h + 4].rearrange("p b g d -> p (b g d)"),
-                in_=seg_grouped[:, 4 * h : 4 * h + 4].rearrange("p b g d t -> p (b g d t)"),
-            )
-
-        for u in range(UNITS):
-            b, c = divmod(u, 2)
-            if u + 5 < UNITS:
-                load_w(u + 5, 1)
-            w_sb = w_tiles.pop(u)
-            d_sb = dpool.tile([P, ROWS, N], BF16, name="d_sb")
-            sums = small.tile([P, ROWS], F32, name="sums")
-            rinv = small.tile([P, ROWS], F32, name="rinv")
-            for j in range(ROWS):
+        def emit(name, arg, engine):
+            if name == "LW":
+                r, n = arg
+                if r % 4 == 0:
+                    w_sb = wpool.tile([P, 4, N], BF16, name="w_sb")
+                    for i in range(4):
+                        w_of[r + i] = w_sb[:, i, :]
+                    w_of[("tile", r)] = w_sb
+                w_sb = w_of[("tile", r - r % 4)]
+                nc.sync.dma_start(
+                    out=w_sb[:, r % 4 : r % 4 + n, :], in_=w_v[r // 8][:, r % 8 : r % 8 + n, :]
+                )
+            elif name == "LS":
+                nc.sync.dma_start(out=seg_sb[:, arg, :], in_=seg_v[arg])
+            elif name == "ST":
+                seg_bank_of[arg] = transpose_rows(seg_sb[:, arg, :])
+            elif name == "SC":
+                copy_on(engine, seg_grouped[:, arg], seg_bank_of[arg])
+            elif name == "SQ":
+                nc.vector.quantize_mx(
+                    out=seg_codes[:, arg].rearrange("p g d -> p (g d)").bitcast(FP8X4),
+                    scales=seg_scales[:, arg].rearrange("p g d -> p (g d)"),
+                    in_=seg_grouped[:, arg].rearrange("p g d t -> p (g d t)"),
+                )
+            elif name == "A":
+                g = group_of[arg]
+                first, size = groups[g]
+                if arg == first:
+                    d_of[g] = dpool.tile([P, size, N], BF16, name="d_sb")
+                    sums_of[g] = small.tile([P, size], F32, name="sums")
                 nc.vector.scalar_tensor_tensor(
-                    out=d_sb[:, j, :],
-                    in0=w_sb[:, j, :],
+                    out=d_of[g][:, arg - first, :],
+                    in0=w_of[arg],
                     scalar=THRESH,
-                    in1=w_sb[:, j, :],
+                    in1=w_of[arg],
                     op0=ALU.is_gt,
                     op1=ALU.mult,
-                    accum_out=sums[:, j : j + 1],
+                    accum_out=sums_of[g][:, arg - first : arg - first + 1],
                 )
-            nc.vector.reciprocal(rinv[:], sums[:])
-            grouped = gpool.tile([P, 2, ROWS * P, 4], BF16, name="grouped", align_bytes=64)
-            for j in range(ROWS):
-                if j in SCALE_ON_SCALAR:
-                    nc.scalar.activation(
-                        out=d_sb[:, j, :], in_=d_sb[:, j, :], func=ACT.Copy, scale=rinv[:, j : j + 1]
-                    )
+            elif name == "R":
+                rinv_of[arg] = small.tile([P, groups[arg][1]], F32, name="rinv")
+                nc.vector.reciprocal(rinv_of[arg][:], sums_of[arg][:])
+            elif name == "B":
+                g = group_of[arg]
+                j = arg - groups[g][0]
+                rows = d_of[g][:, j, :]
+                if engine == "act":
+                    nc.scalar.activation(out=rows, in_=rows, func=ACT.Copy, scale=rinv_of[g][:, j : j + 1])
                 else:
-                    nc.vector.tensor_scalar_mul(
-                        out=d_sb[:, j, :], in0=d_sb[:, j, :], scalar1=rinv[:, j : j + 1]
+                    nc.vector.tensor_scalar_mul(out=rows, in0=rows, scalar1=rinv_of[g][:, j : j + 1])
+            elif name == "T":
+                g = group_of[arg]
+                bank_of[arg] = transpose_rows(d_of[g][:, arg - groups[g][0], :])
+            elif name == "C":
+                g = group_of[arg]
+                first, size = groups[g]
+                if g not in grouped_of:
+                    grouped_of[g] = gpool.tile([P, 2, size * P, 4], BF16, name="grouped", align_bytes=64)
+                j = arg - first
+                copy_on(engine, grouped_of[g][:, :, j * P : (j + 1) * P, :], bank_of[arg])
+            elif name == "Q":
+                width = 2 * groups[arg][1] * P
+                codes = qpool.tile([P, width], U32, name="codes", align_bytes=64)
+                scales = qpool.tile([P, width], U8, name="scales", align_bytes=64)
+                nc.vector.quantize_mx(
+                    out=codes[:].bitcast(FP8X4),
+                    scales=scales[:],
+                    in_=grouped_of[arg][:].rearrange("p g m t -> p (g m t)"),
+                )
+                codes_of[arg] = (codes, scales)
+            elif name == "M":
+                first, size = groups[arg]
+                codes, scales = codes_of[arg]
+                acc = apsum.tile([P, size * P], F32, name="acc")
+                for h in range(2):
+                    cols = slice(h * size * P, (h + 1) * size * P)
+                    nc.tensor.matmul_mx(
+                        out=acc[:],
+                        lhsT=seg_codes[:, first // 8, h, :].bitcast(FP8X4),
+                        lhsT_scale=seg_scales[:, first // 8, h, :],
+                        rhs=codes[:, cols].bitcast(FP8X4),
+                        rhs_scale=scales[:, cols],
+                        start=(h == 0),
+                        stop=(h == 1),
                     )
-            for j in range(ROWS):
-                nc.scalar.copy(
-                    out=grouped[:, :, j * P : (j + 1) * P, :], in_=transpose_rows(d_sb[:, j, :])
-                )
-            codes = qpool.tile([P, 2 * ROWS * P], U32, name="codes", align_bytes=64)
-            scales = qpool.tile([P, 2 * ROWS * P], U8, name="scales", align_bytes=64)
-            nc.vector.quantize_mx(
-                out=codes[:].bitcast(FP8X4),
-                scales=scales[:],
-                in_=grouped[:].rearrange("p g m t -> p (g m t)"),
-            )
-            acc = apsum.tile([P, ROWS * P], F32, name="acc")
-            for g in range(2):
-                cols = slice(g * ROWS * P, (g + 1) * ROWS * P)
-                nc.tensor.matmul_mx(
-                    out=acc[:],
-                    lhsT=seg_codes[:, b, g, :].bitcast(FP8X4),
-                    lhsT_scale=seg_scales[:, b, g, :],
-                    rhs=codes[:, cols].bitcast(FP8X4),
-                    rhs_scale=scales[:, cols],
-                    start=(g == 0),
-                    stop=(g == 1),
-                )
-            o_sb = opool.tile([P, ROWS * P], F32, name="o_sb")
-            nc.scalar.copy(out=o_sb[:], in_=acc[:])
-            nc.sync.dma_start(out=out_v[b][:, c * ROWS * P : (c + 1) * ROWS * P], in_=o_sb[:])
+                acc_of[arg] = acc
+            elif name == "X":
+                o_of[arg] = opool.tile([P, groups[arg][1] * P], F32, name="o_sb")
+                copy_on(engine, o_of[arg][:], acc_of[arg][:])
+            elif name == "O":
+                first, size = groups[arg]
+                lo = (first % 8) * P
+                nc.sync.dma_start(out=out_v[first // 8][:, lo : lo + size * P], in_=o_of[arg][:])
+
+        with tc.manual_schedule():
+            for name, arg, engine in make_plan(make_cfg()):
+                emit(name, arg, engine)

@@ -23,16 +23,16 @@ def make_cfg():
         "prefetch": 6,
         "seg_tick": [0, 1, 2, 3, 4, 5, 6, 7],
         "lag_b": 2,
-        "lag_c": 1,
-        "lag_q": 2,
+        "lag_c": 2,
+        "lag_q": 3,
         "lag_x": 1,
-        "b_on_act": set(r for r in range(56) if r % 4 == 3 or r % 12 == 1),
-        "c_on_dve": set([60, 62]),
+        "b_on_act": set(r for r in range(48) if r % 8 in (1, 3, 7)),
+        "c_on_dve": set([62]),
         "x_on_dve": set([]),
     }
 
 
-GROUP_SIZES = [4] * 15 + [2, 2]
+GROUP_SIZES = [4] * 14 + [2, 2, 2, 2]
 
 
 def make_groups():
@@ -117,6 +117,8 @@ def tile_regu_diff_t_kernel(tc, seg, W, out):
 
         ident = const.tile([P, P], BF16)
         make_identity(nc, ident[:])
+        ident_f32 = const.tile([P, P], F32)
+        make_identity(nc, ident_f32[:])
         seg_sb = const.tile([P, BS, N], BF16)
         seg_grouped = const.tile([P, BS, 2, DC, 4], BF16, align_bytes=64)
         seg_codes = const.tile([P, BS, 2, DC], U32, align_bytes=64)
@@ -136,8 +138,16 @@ def tile_regu_diff_t_kernel(tc, seg, W, out):
         def transpose_rows(src):
             bank = tpsum.tile([P, 8, P], BF16, name="bank")
             for k in range(8):
-                nc.tensor.transpose(bank[:, k, :], src[:, k * P : (k + 1) * P], ident[:])
+                lo = (k // 2) * 2 * P + k % 2
+                nc.tensor.transpose(bank[:, k, :], src[:, lo : lo + 2 * P - 1 : 2], ident[:])
             return bank[:].rearrange("p (g t) m -> p g m t", g=2)
+
+        def transpose_words(src):
+            bank = tpsum.tile([P, 4, P], F32, name="bank")
+            words = src.bitcast(F32)
+            for k in range(4):
+                nc.tensor.transpose(bank[:, k, :], words[:, k * P : (k + 1) * P], ident_f32[:])
+            return bank[:].rearrange("p (g u) d -> p g d u", g=2)
 
         def copy_on(engine, dst, src):
             if engine == "act":
@@ -160,9 +170,9 @@ def tile_regu_diff_t_kernel(tc, seg, W, out):
             elif name == "LS":
                 nc.sync.dma_start(out=seg_sb[:, arg, :], in_=seg_v[arg])
             elif name == "ST":
-                seg_bank_of[arg] = transpose_rows(seg_sb[:, arg, :])
+                seg_bank_of[arg] = transpose_words(seg_sb[:, arg, :])
             elif name == "SC":
-                copy_on(engine, seg_grouped[:, arg], seg_bank_of[arg])
+                copy_on(engine, seg_grouped[:, arg].rearrange("p g d t -> p g (d t)").bitcast(F32).rearrange("p g (d u) -> p g d u", u=2), seg_bank_of[arg])
             elif name == "SQ":
                 nc.vector.quantize_mx(
                     out=seg_codes[:, arg].rearrange("p g d -> p (g d)").bitcast(FP8X4),

@@ -73,6 +73,8 @@ def make_plan(cfg):
         put(t0 + 3, ("SQ", b, "dve"))
     for r in range(n_rows):
         put(r, ("A", r, "dve"))
+    for tick in range(6, 72, 1):
+        put(tick, ("WARM", tick, "pe"))
     for g, (first, size) in enumerate(groups):
         last = first + size - 1
         put(last + 1, ("R", g, "dve"))
@@ -87,7 +89,7 @@ def make_plan(cfg):
         put(tq, ("M", g, "pe"))
         put(tq + cfg["lag_x"], ("X", g, "dve" if g in cfg["x_on_dve"] else "act"))
         put(tq + cfg["lag_x"], ("O", g, "sync"))
-    rank = {"LW": 0, "LS": 0, "A": 1, "R": 2, "SQ": 3, "B": 4, "ST": 5, "T": 5, "SC": 6, "C": 6, "Q": 7, "M": 8, "X": 9, "O": 10}
+    rank = {"LW": 0, "LS": 0, "A": 1, "R": 2, "SQ": 3, "B": 4, "ST": 5, "T": 5, "WARM": 5.5, "SC": 6, "C": 6, "Q": 7, "M": 8, "X": 9, "O": 10}
     for tick in sorted(at):
         order.extend(sorted(at[tick], key=lambda e: rank[e[0]]))
     return order
@@ -112,7 +114,8 @@ def tile_regu_diff_t_kernel(tc, seg, W, out):
         gpool = ctx.enter_context(tc.tile_pool(name="gpool", bufs=5))
         qpool = ctx.enter_context(tc.tile_pool(name="qpool", bufs=3))
         opool = ctx.enter_context(tc.tile_pool(name="opool", bufs=3))
-        tpsum = ctx.enter_context(tc.psum_pool(name="tpsum", bufs=6))
+        tpsum = ctx.enter_context(tc.psum_pool(name="tpsum", bufs=5))
+        wpsum = ctx.enter_context(tc.psum_pool(name="wpsum", bufs=1))
         apsum = ctx.enter_context(tc.psum_pool(name="apsum", bufs=2))
 
         ident = const.tile([P, P], BF16)
@@ -244,6 +247,17 @@ def tile_regu_diff_t_kernel(tc, seg, W, out):
             elif name == "X":
                 o_of[arg] = opool.tile([P, groups[arg][1] * P], F32, name="o_sb")
                 copy_on(engine, o_of[arg][:], acc_of[arg][:])
+            elif name == "WARM":
+                idle = wpsum.tile([P, 4 * P], F32, name="idle")
+                nc.tensor.matmul_mx(
+                    out=idle[:],
+                    lhsT=seg_codes[:, 0, 0, :].bitcast(FP8X4),
+                    lhsT_scale=seg_scales[:, 0, 0, :],
+                    rhs=seg_codes[:, 0:2].rearrange("p b g d -> p (b g d)").bitcast(FP8X4),
+                    rhs_scale=seg_scales[:, 0:2].rearrange("p b g d -> p (b g d)"),
+                    start=True,
+                    stop=True,
+                )
             elif name == "O":
                 first, size = groups[arg]
                 lo = (first % 8) * P

@@ -23,16 +23,16 @@ def make_cfg():
         "prefetch": 6,
         "seg_tick": [0, 1, 2, 3, 4, 5, 6, 7],
         "lag_b": 2,
-        "lag_c": 2,
-        "lag_q": 3,
+        "lag_c": 1,
+        "lag_q": 2,
         "lag_x": 1,
-        "b_on_act": set(r for r in range(48) if r % 8 in (1, 3, 7)),
-        "c_on_dve": set([62]),
+        "b_on_act": set([0, 2] + [r for r in range(52) if r % 8 in (1, 3, 7)]),
+        "c_on_dve": set([]),
         "x_on_dve": set([]),
     }
 
 
-GROUP_SIZES = [4] * 14 + [2, 2, 2, 2]
+GROUP_SIZES = [2, 2, 2, 2] + [4] * 12 + [2, 2, 2, 1, 1]
 
 
 def make_groups():
@@ -73,8 +73,6 @@ def make_plan(cfg):
         put(t0 + 3, ("SQ", b, "dve"))
     for r in range(n_rows):
         put(r, ("A", r, "dve"))
-    for tick in range(6, 72, 1):
-        put(tick, ("WARM", tick, "pe"))
     for g, (first, size) in enumerate(groups):
         last = first + size - 1
         put(last + 1, ("R", g, "dve"))
@@ -89,7 +87,7 @@ def make_plan(cfg):
         put(tq, ("M", g, "pe"))
         put(tq + cfg["lag_x"], ("X", g, "dve" if g in cfg["x_on_dve"] else "act"))
         put(tq + cfg["lag_x"], ("O", g, "sync"))
-    rank = {"LW": 0, "LS": 0, "A": 1, "R": 2, "SQ": 3, "B": 4, "ST": 5, "T": 5, "WARM": 5.5, "SC": 6, "C": 6, "Q": 7, "M": 8, "X": 9, "O": 10}
+    rank = {"LW": 0, "LS": 0, "A": 1, "R": 2, "SQ": 3, "B": 4, "ST": 5, "T": 5, "SC": 6, "C": 6, "Q": 7, "M": 8, "X": 9, "O": 10}
     for tick in sorted(at):
         order.extend(sorted(at[tick], key=lambda e: rank[e[0]]))
     return order
@@ -114,8 +112,7 @@ def tile_regu_diff_t_kernel(tc, seg, W, out):
         gpool = ctx.enter_context(tc.tile_pool(name="gpool", bufs=5))
         qpool = ctx.enter_context(tc.tile_pool(name="qpool", bufs=3))
         opool = ctx.enter_context(tc.tile_pool(name="opool", bufs=3))
-        tpsum = ctx.enter_context(tc.psum_pool(name="tpsum", bufs=5))
-        wpsum = ctx.enter_context(tc.psum_pool(name="wpsum", bufs=1))
+        tpsum = ctx.enter_context(tc.psum_pool(name="tpsum", bufs=6))
         apsum = ctx.enter_context(tc.psum_pool(name="apsum", bufs=2))
 
         ident = const.tile([P, P], BF16)
@@ -247,17 +244,6 @@ def tile_regu_diff_t_kernel(tc, seg, W, out):
             elif name == "X":
                 o_of[arg] = opool.tile([P, groups[arg][1] * P], F32, name="o_sb")
                 copy_on(engine, o_of[arg][:], acc_of[arg][:])
-            elif name == "WARM":
-                idle = wpsum.tile([P, 4 * P], F32, name="idle")
-                nc.tensor.matmul_mx(
-                    out=idle[:],
-                    lhsT=seg_codes[:, 0, 0, :].bitcast(FP8X4),
-                    lhsT_scale=seg_scales[:, 0, 0, :],
-                    rhs=seg_codes[:, 0:2].rearrange("p b g d -> p (b g d)").bitcast(FP8X4),
-                    rhs_scale=seg_scales[:, 0:2].rearrange("p b g d -> p (b g d)"),
-                    start=True,
-                    stop=True,
-                )
             elif name == "O":
                 first, size = groups[arg]
                 lo = (first % 8) * P

@@ -11,105 +11,49 @@ FP8X4 = mybir.dt.float8_e4m3fn_x4
 ALU = mybir.AluOpType
 ACT = mybir.ActivationFunctionType
 
-BS = 8
-DC = 128
+BATCH = 8
+CHANNELS = 128
 N = 1024
 P = 128
-THRESH = 0.85
-FLOPS = 2 * BS * DC * N * N
+THRESHOLD = 0.85
+FLOPS = 2 * BATCH * CHANNELS * N * N
 
-def make_cfg():
-    return {
-        "prefetch": 6,
-        "seg_tick": [0, 1, 2, 3, 4, 5, 6, 7],
-        "lag_b": 2,
-        "lag_c": 1,
-        "lag_q": 2,
-        "lag_x": 1,
-        "b_on_act": set([0, 2] + [r for r in range(52) if r % 8 in (1, 3, 7)]),
-        "c_on_dve": set([]),
-        "x_on_dve": set([]),
-    }
+PASSES = 2
+PACK = 4
+ROW_TILES = BATCH * N // P
+TILES_PER_BATCH = N // P
+PAIRS = ROW_TILES // 2
+PAIR_COLS = 2 * P
+PAIRS_PER_BATCH = TILES_PER_BATCH // 2
+AHEAD = 24
 
-
-GROUP_SIZES = [2, 2, 2, 2] + [4] * 12 + [2, 2, 2, 1, 1]
-
-
-def make_groups():
-    groups = []
-    first = 0
-    for size in GROUP_SIZES:
-        groups.append((first, size))
-        first += size
-    return groups
+NORMALISE_AFTER = 3
+REGROUP_AFTER = 5
+QUANTISE_AFTER = 9
+LEAVE_AFTER = 10
+STEPS = 2 * (PAIRS - 1) + LEAVE_AFTER + 1
 
 
-def make_plan(cfg):
-    groups = make_groups()
-    n_rows = 64
-    group_of = {}
-    for g, (first, size) in enumerate(groups):
-        for i in range(size):
-            group_of[first + i] = g
-    at = {}
+def normalised_on_scalar(r):
+    return r % 3 == 0 and r < ROW_TILES - TILES_PER_BATCH
 
-    def put(tick, entry):
-        if tick not in at:
-            at[tick] = []
-        at[tick].append(entry)
 
-    order = []
-    for r in range(8):
-        order.append(("LW", (r, 1), "sync"))
-        order.append(("LS", r, "sync"))
-    for r in range(8, cfg["prefetch"] * 4, 4):
-        order.append(("LW", (r, 4), "sync"))
-    for r in range(cfg["prefetch"] * 4, n_rows, 4):
-        put(r - cfg["prefetch"] * 4 + 4, ("LW", (r, 4), "sync"))
-    for b in range(8):
-        t0 = cfg["seg_tick"][b]
-        put(t0, ("ST", b, "pe"))
-        put(t0 + 1, ("SC", b, "act"))
-        put(t0 + 3, ("SQ", b, "dve"))
-    for r in range(n_rows):
-        put(r, ("A", r, "dve"))
-    for g, (first, size) in enumerate(groups):
-        last = first + size - 1
-        put(last + 1, ("R", g, "dve"))
-        for i in range(size):
-            r = first + i
-            tb = last + cfg["lag_b"] + i
-            put(tb, ("B", r, "act" if r in cfg["b_on_act"] else "dve"))
-            put(tb, ("T", r, "pe"))
-            put(tb + cfg["lag_c"], ("C", r, "dve" if r in cfg["c_on_dve"] else "act"))
-        tq = last + cfg["lag_b"] + size - 1 + cfg["lag_c"] + cfg["lag_q"]
-        put(tq, ("Q", g, "dve"))
-        put(tq, ("M", g, "pe"))
-        put(tq + cfg["lag_x"], ("X", g, "dve" if g in cfg["x_on_dve"] else "act"))
-        put(tq + cfg["lag_x"], ("O", g, "sync"))
-    rank = {"LW": 0, "LS": 0, "A": 1, "R": 2, "SQ": 3, "B": 4, "ST": 5, "T": 5, "SC": 6, "C": 6, "Q": 7, "M": 8, "X": 9, "O": 10}
-    for tick in sorted(at):
-        order.extend(sorted(at[tick], key=lambda e: rank[e[0]]))
-    return order
+def regrouped_on_vector(r):
+    return r == ROW_TILES - 2
 
 
 def tile_regu_diff_t_kernel(tc, seg, W, out):
     nc = tc.nc
     seg_v = seg.rearrange("b d r c -> b d (r c)")
-    w_v = W.rearrange("b (j p) n -> b p j n", p=P)
+    w_v = W.rearrange("b (j p) n -> (b j) p n", p=P)
     out_v = out.rearrange("b d r c -> b d (r c)")
-    groups = make_groups()
-    group_of = {}
-    for g, (first, size) in enumerate(groups):
-        for i in range(size):
-            group_of[first + i] = g
 
     with ExitStack() as ctx:
         const = ctx.enter_context(tc.tile_pool(name="const", bufs=1))
-        wpool = ctx.enter_context(tc.tile_pool(name="wpool", bufs=make_cfg()["prefetch"]))
-        dpool = ctx.enter_context(tc.tile_pool(name="dpool", bufs=4))
+        wpool = ctx.enter_context(tc.tile_pool(name="wpool", bufs=AHEAD))
+        dpool = ctx.enter_context(tc.tile_pool(name="dpool", bufs=8))
         small = ctx.enter_context(tc.tile_pool(name="small", bufs=6))
-        gpool = ctx.enter_context(tc.tile_pool(name="gpool", bufs=5))
+        gpool = ctx.enter_context(tc.tile_pool(name="gpool", bufs=6))
         qpool = ctx.enter_context(tc.tile_pool(name="qpool", bufs=3))
         opool = ctx.enter_context(tc.tile_pool(name="opool", bufs=3))
         tpsum = ctx.enter_context(tc.psum_pool(name="tpsum", bufs=6))
@@ -119,136 +63,159 @@ def tile_regu_diff_t_kernel(tc, seg, W, out):
         make_identity(nc, ident[:])
         ident_f32 = const.tile([P, P], F32)
         make_identity(nc, ident_f32[:])
-        seg_sb = const.tile([P, BS, N], BF16)
-        seg_grouped = const.tile([P, BS, 2, DC, 4], BF16, align_bytes=64)
-        seg_codes = const.tile([P, BS, 2, DC], U32, align_bytes=64)
-        seg_scales = const.tile([P, BS, 2, DC], U8, align_bytes=64)
 
-        w_of = {}
-        d_of = {}
-        sums_of = {}
-        rinv_of = {}
-        bank_of = {}
-        seg_bank_of = {}
-        grouped_of = {}
-        codes_of = {}
-        acc_of = {}
-        o_of = {}
+        seg_sb = const.tile([P, BATCH, N], BF16)
+        seg_grouped = const.tile([P, BATCH, PASSES, CHANNELS, PACK], BF16, align_bytes=64)
+        seg_codes = const.tile([P, BATCH, PASSES, CHANNELS], U32, align_bytes=64)
+        seg_scales = const.tile([P, BATCH, PASSES, CHANNELS], U8, align_bytes=64)
 
-        def transpose_rows(src):
-            bank = tpsum.tile([P, 8, P], BF16, name="bank")
-            for k in range(8):
-                lo = (k // 2) * 2 * P + k % 2
-                nc.tensor.transpose(bank[:, k, :], src[:, lo : lo + 2 * P - 1 : 2], ident[:])
-            return bank[:].rearrange("p (g t) m -> p g m t", g=2)
+        w_rows = {}
+        d_rows = {}
+        banks = {}
+        seg_banks = {}
+        sums = {}
+        scales_of_rows = {}
+        grouped = {}
+        quantised = {}
+        products = {}
+        results = {}
 
-        def transpose_words(src):
-            bank = tpsum.tile([P, 4, P], F32, name="bank")
-            words = src.bitcast(F32)
-            for k in range(4):
+        def load_rows(r):
+            w_rows[r] = wpool.tile([P, N], BF16, name="w_rows")
+            nc.sync.dma_start(out=w_rows[r][:], in_=w_v[r])
+
+        def load_seg(b):
+            nc.sync.dma_start(out=seg_sb[:, b, :], in_=seg_v[b])
+
+        def transpose_seg(b):
+            words = seg_sb[:, b, :].bitcast(F32)
+            bank = tpsum.tile([P, PASSES * 2, CHANNELS], F32, name="bank")
+            for k in range(PASSES * 2):
                 nc.tensor.transpose(bank[:, k, :], words[:, k * P : (k + 1) * P], ident_f32[:])
-            return bank[:].rearrange("p (g u) d -> p g d u", g=2)
+            seg_banks[b] = bank
 
-        def copy_on(engine, dst, src):
-            if engine == "act":
-                nc.scalar.copy(out=dst, in_=src)
+        def regroup_seg(b):
+            nc.scalar.copy(
+                out=seg_grouped[:, b]
+                .rearrange("p c d t -> p c (d t)")
+                .bitcast(F32)
+                .rearrange("p c (d u) -> p c d u", u=2),
+                in_=seg_banks[b][:].rearrange("p (c u) d -> p c d u", u=2),
+            )
+
+        def quantise_seg(b):
+            nc.vector.quantize_mx(
+                out=seg_codes[:, b].rearrange("p c d -> p (c d)").bitcast(FP8X4),
+                scales=seg_scales[:, b].rearrange("p c d -> p (c d)"),
+                in_=seg_grouped[:, b].rearrange("p c d t -> p (c d t)"),
+            )
+
+        def threshold_and_sum(r):
+            if r % 2 == 0:
+                sums[r // 2] = small.tile([P, 2], F32, name="sums")
+            d_rows[r] = dpool.tile([P, N], BF16, name="d_rows")
+            nc.vector.scalar_tensor_tensor(
+                out=d_rows[r][:],
+                in0=w_rows[r][:],
+                scalar=THRESHOLD,
+                in1=w_rows[r][:],
+                op0=ALU.is_gt,
+                op1=ALU.mult,
+                accum_out=sums[r // 2][:, r % 2 : r % 2 + 1],
+            )
+
+        def invert_sums(i):
+            scales_of_rows[i] = small.tile([P, 2], F32, name="scales_of_rows")
+            nc.vector.reciprocal(scales_of_rows[i][:], sums[i][:])
+
+        def normalise(r):
+            rows = d_rows[r][:]
+            scale = scales_of_rows[r // 2][:, r % 2 : r % 2 + 1]
+            if normalised_on_scalar(r):
+                nc.scalar.activation(out=rows, in_=rows, func=ACT.Copy, scale=scale)
             else:
-                nc.vector.tensor_copy(out=dst, in_=src)
+                nc.vector.tensor_scalar_mul(out=rows, in0=rows, scalar1=scale)
 
-        def emit(name, arg, engine):
-            if name == "LW":
-                r, n = arg
-                if r % 4 == 0:
-                    w_sb = wpool.tile([P, 4, N], BF16, name="w_sb")
-                    for i in range(4):
-                        w_of[r + i] = w_sb[:, i, :]
-                    w_of[("tile", r)] = w_sb
-                w_sb = w_of[("tile", r - r % 4)]
-                nc.sync.dma_start(
-                    out=w_sb[:, r % 4 : r % 4 + n, :], in_=w_v[r // 8][:, r % 8 : r % 8 + n, :]
+        def transpose_rows(r):
+            bank = tpsum.tile([P, PASSES * PACK, P], BF16, name="bank")
+            for k in range(PASSES * PACK):
+                first = 2 * P * (k // 2) + k % 2
+                nc.tensor.transpose(bank[:, k, :], d_rows[r][:, first : first + 2 * P - 1 : 2], ident[:])
+            banks[r] = bank
+
+        def regroup(r):
+            if r % 2 == 0:
+                grouped[r // 2] = gpool.tile([P, PASSES, PAIR_COLS, PACK], BF16, name="grouped", align_bytes=64)
+            dst = grouped[r // 2][:, :, (r % 2) * P : (r % 2 + 1) * P, :]
+            src = banks[r][:].rearrange("p (c t) m -> p c m t", t=PACK)
+            if regrouped_on_vector(r):
+                nc.vector.tensor_copy(out=dst, in_=src)
+            else:
+                nc.scalar.copy(out=dst, in_=src)
+
+        def quantise(i):
+            codes = qpool.tile([P, PASSES * PAIR_COLS], U32, name="codes", align_bytes=64)
+            scales = qpool.tile([P, PASSES * PAIR_COLS], U8, name="scales", align_bytes=64)
+            nc.vector.quantize_mx(
+                out=codes[:].bitcast(FP8X4),
+                scales=scales[:],
+                in_=grouped[i][:].rearrange("p c m t -> p (c m t)"),
+            )
+            quantised[i] = (codes, scales)
+
+        def multiply(i):
+            b = i // PAIRS_PER_BATCH
+            codes, scales = quantised[i]
+            products[i] = apsum.tile([P, PAIR_COLS], F32, name="products")
+            for c in range(PASSES):
+                cols = slice(c * PAIR_COLS, (c + 1) * PAIR_COLS)
+                nc.tensor.matmul_mx(
+                    out=products[i][:],
+                    lhsT=seg_codes[:, b, c, :].bitcast(FP8X4),
+                    lhsT_scale=seg_scales[:, b, c, :],
+                    rhs=codes[:, cols].bitcast(FP8X4),
+                    rhs_scale=scales[:, cols],
+                    start=(c == 0),
+                    stop=(c == PASSES - 1),
                 )
-            elif name == "LS":
-                nc.sync.dma_start(out=seg_sb[:, arg, :], in_=seg_v[arg])
-            elif name == "ST":
-                seg_bank_of[arg] = transpose_words(seg_sb[:, arg, :])
-            elif name == "SC":
-                copy_on(engine, seg_grouped[:, arg].rearrange("p g d t -> p g (d t)").bitcast(F32).rearrange("p g (d u) -> p g d u", u=2), seg_bank_of[arg])
-            elif name == "SQ":
-                nc.vector.quantize_mx(
-                    out=seg_codes[:, arg].rearrange("p g d -> p (g d)").bitcast(FP8X4),
-                    scales=seg_scales[:, arg].rearrange("p g d -> p (g d)"),
-                    in_=seg_grouped[:, arg].rearrange("p g d t -> p (g d t)"),
-                )
-            elif name == "A":
-                g = group_of[arg]
-                first, size = groups[g]
-                if arg == first:
-                    d_of[g] = dpool.tile([P, size, N], BF16, name="d_sb")
-                    sums_of[g] = small.tile([P, size], F32, name="sums")
-                nc.vector.scalar_tensor_tensor(
-                    out=d_of[g][:, arg - first, :],
-                    in0=w_of[arg],
-                    scalar=THRESH,
-                    in1=w_of[arg],
-                    op0=ALU.is_gt,
-                    op1=ALU.mult,
-                    accum_out=sums_of[g][:, arg - first : arg - first + 1],
-                )
-            elif name == "R":
-                rinv_of[arg] = small.tile([P, groups[arg][1]], F32, name="rinv")
-                nc.vector.reciprocal(rinv_of[arg][:], sums_of[arg][:])
-            elif name == "B":
-                g = group_of[arg]
-                j = arg - groups[g][0]
-                rows = d_of[g][:, j, :]
-                if engine == "act":
-                    nc.scalar.activation(out=rows, in_=rows, func=ACT.Copy, scale=rinv_of[g][:, j : j + 1])
-                else:
-                    nc.vector.tensor_scalar_mul(out=rows, in0=rows, scalar1=rinv_of[g][:, j : j + 1])
-            elif name == "T":
-                g = group_of[arg]
-                bank_of[arg] = transpose_rows(d_of[g][:, arg - groups[g][0], :])
-            elif name == "C":
-                g = group_of[arg]
-                first, size = groups[g]
-                if g not in grouped_of:
-                    grouped_of[g] = gpool.tile([P, 2, size * P, 4], BF16, name="grouped", align_bytes=64)
-                j = arg - first
-                copy_on(engine, grouped_of[g][:, :, j * P : (j + 1) * P, :], bank_of[arg])
-            elif name == "Q":
-                width = 2 * groups[arg][1] * P
-                codes = qpool.tile([P, width], U32, name="codes", align_bytes=64)
-                scales = qpool.tile([P, width], U8, name="scales", align_bytes=64)
-                nc.vector.quantize_mx(
-                    out=codes[:].bitcast(FP8X4),
-                    scales=scales[:],
-                    in_=grouped_of[arg][:].rearrange("p g m t -> p (g m t)"),
-                )
-                codes_of[arg] = (codes, scales)
-            elif name == "M":
-                first, size = groups[arg]
-                codes, scales = codes_of[arg]
-                acc = apsum.tile([P, size * P], F32, name="acc")
-                for h in range(2):
-                    cols = slice(h * size * P, (h + 1) * size * P)
-                    nc.tensor.matmul_mx(
-                        out=acc[:],
-                        lhsT=seg_codes[:, first // 8, h, :].bitcast(FP8X4),
-                        lhsT_scale=seg_scales[:, first // 8, h, :],
-                        rhs=codes[:, cols].bitcast(FP8X4),
-                        rhs_scale=scales[:, cols],
-                        start=(h == 0),
-                        stop=(h == 1),
-                    )
-                acc_of[arg] = acc
-            elif name == "X":
-                o_of[arg] = opool.tile([P, groups[arg][1] * P], F32, name="o_sb")
-                copy_on(engine, o_of[arg][:], acc_of[arg][:])
-            elif name == "O":
-                first, size = groups[arg]
-                lo = (first % 8) * P
-                nc.sync.dma_start(out=out_v[first // 8][:, lo : lo + size * P], in_=o_of[arg][:])
+
+        def leave_psum(i):
+            results[i] = opool.tile([P, PAIR_COLS], F32, name="results")
+            nc.scalar.copy(out=results[i][:], in_=products[i][:])
+
+        def store(i):
+            first = (i % PAIRS_PER_BATCH) * PAIR_COLS
+            nc.sync.dma_start(out=out_v[i // PAIRS_PER_BATCH][:, first : first + PAIR_COLS], in_=results[i][:])
 
         with tc.manual_schedule():
-            for name, arg, engine in make_plan(make_cfg()):
-                emit(name, arg, engine)
+            for b in range(BATCH):
+                load_rows(b)
+                load_seg(b)
+            for r in range(BATCH, AHEAD):
+                load_rows(r)
+
+            for s in range(STEPS):
+                if s < ROW_TILES:
+                    threshold_and_sum(s)
+                if s + AHEAD < ROW_TILES:
+                    load_rows(s + AHEAD)
+                if s % 2 == 0 and 0 <= s // 2 - 1 < PAIRS:
+                    invert_sums(s // 2 - 1)
+                if 0 <= s - 3 < BATCH:
+                    quantise_seg(s - 3)
+                if 0 <= s - NORMALISE_AFTER < ROW_TILES:
+                    normalise(s - NORMALISE_AFTER)
+                if s < BATCH:
+                    transpose_seg(s)
+                if 0 <= s - NORMALISE_AFTER < ROW_TILES:
+                    transpose_rows(s - NORMALISE_AFTER)
+                if 0 <= s - 1 < BATCH:
+                    regroup_seg(s - 1)
+                if 0 <= s - REGROUP_AFTER < ROW_TILES:
+                    regroup(s - REGROUP_AFTER)
+                if (s - QUANTISE_AFTER) % 2 == 0 and 0 <= (s - QUANTISE_AFTER) // 2 < PAIRS:
+                    quantise((s - QUANTISE_AFTER) // 2)
+                    multiply((s - QUANTISE_AFTER) // 2)
+                if (s - LEAVE_AFTER) % 2 == 0 and 0 <= (s - LEAVE_AFTER) // 2 < PAIRS:
+                    leave_psum((s - LEAVE_AFTER) // 2)
+                    store((s - LEAVE_AFTER) // 2)

@@ -22,20 +22,37 @@ PASSES = 2
 PACK = 4
 ROW_TILES = BATCH * N // P
 TILES_PER_BATCH = N // P
-PAIRS = ROW_TILES // 2
-PAIR_COLS = 2 * P
-PAIRS_PER_BATCH = TILES_PER_BATCH // 2
-AHEAD = 24
+LOAD_TILES = 4
+LOADS_AHEAD = 6
 
-NORMALISE_AFTER = 3
-REGROUP_AFTER = 5
-QUANTISE_AFTER = 9
-LEAVE_AFTER = 10
-STEPS = 2 * (PAIRS - 1) + LEAVE_AFTER + 1
+GROUP_SIZES = [4] * 14 + [2] * 4
+
+REGROUP_LAG = 2
+QUANTISE_LAG = 3
+LEAVE_LAG = 1
+
+
+def make_groups():
+    groups = []
+    for size in GROUP_SIZES:
+        groups.append((sum(GROUP_SIZES[: len(groups)]), size))
+    return groups
+
+
+def invert_step(first, size):
+    return first + size
+
+
+def normalise_step(first, size, r):
+    return invert_step(first, size) + 1 + (r - first)
+
+
+def quantise_step(first, size):
+    return normalise_step(first, size, first + size - 1) + REGROUP_LAG + QUANTISE_LAG
 
 
 def normalised_on_scalar(r):
-    return r % 3 == 0 and r < ROW_TILES - TILES_PER_BATCH
+    return r % 8 in (1, 3, 7) and r < ROW_TILES - 2 * TILES_PER_BATCH
 
 
 def regrouped_on_vector(r):
@@ -45,15 +62,21 @@ def regrouped_on_vector(r):
 def tile_regu_diff_t_kernel(tc, seg, W, out):
     nc = tc.nc
     seg_v = seg.rearrange("b d r c -> b d (r c)")
-    w_v = W.rearrange("b (j p) n -> (b j) p n", p=P)
+    w_v = W.rearrange("b (j p) n -> b p j n", p=P)
     out_v = out.rearrange("b d r c -> b d (r c)")
+    groups = make_groups()
+    group_of = {}
+    for first, size in groups:
+        for r in range(first, first + size):
+            group_of[r] = (first, size)
+    steps = quantise_step(*groups[-1]) + LEAVE_LAG + 1
 
     with ExitStack() as ctx:
         const = ctx.enter_context(tc.tile_pool(name="const", bufs=1))
-        wpool = ctx.enter_context(tc.tile_pool(name="wpool", bufs=AHEAD))
-        dpool = ctx.enter_context(tc.tile_pool(name="dpool", bufs=8))
+        wpool = ctx.enter_context(tc.tile_pool(name="wpool", bufs=LOADS_AHEAD))
+        dpool = ctx.enter_context(tc.tile_pool(name="dpool", bufs=4))
         small = ctx.enter_context(tc.tile_pool(name="small", bufs=6))
-        gpool = ctx.enter_context(tc.tile_pool(name="gpool", bufs=6))
+        gpool = ctx.enter_context(tc.tile_pool(name="gpool", bufs=5))
         qpool = ctx.enter_context(tc.tile_pool(name="qpool", bufs=3))
         opool = ctx.enter_context(tc.tile_pool(name="opool", bufs=3))
         tpsum = ctx.enter_context(tc.psum_pool(name="tpsum", bufs=6))
@@ -69,20 +92,26 @@ def tile_regu_diff_t_kernel(tc, seg, W, out):
         seg_codes = const.tile([P, BATCH, PASSES, CHANNELS], U32, align_bytes=64)
         seg_scales = const.tile([P, BATCH, PASSES, CHANNELS], U8, align_bytes=64)
 
-        w_rows = {}
-        d_rows = {}
+        w_tiles = {}
         banks = {}
         seg_banks = {}
+        d_tiles = {}
         sums = {}
-        scales_of_rows = {}
+        inverses = {}
         grouped = {}
         quantised = {}
         products = {}
         results = {}
 
-        def load_rows(r):
-            w_rows[r] = wpool.tile([P, N], BF16, name="w_rows")
-            nc.sync.dma_start(out=w_rows[r][:], in_=w_v[r])
+        def load_rows(r, count):
+            base = r - r % LOAD_TILES
+            if r == base:
+                w_tiles[base] = wpool.tile([P, LOAD_TILES, N], BF16, name="w_sb")
+            j = r % TILES_PER_BATCH
+            nc.sync.dma_start(
+                out=w_tiles[base][:, r - base : r - base + count, :],
+                in_=w_v[r // TILES_PER_BATCH][:, j : j + count, :],
+            )
 
         def load_seg(b):
             nc.sync.dma_start(out=seg_sb[:, b, :], in_=seg_v[b])
@@ -111,66 +140,73 @@ def tile_regu_diff_t_kernel(tc, seg, W, out):
             )
 
         def threshold_and_sum(r):
-            if r % 2 == 0:
-                sums[r // 2] = small.tile([P, 2], F32, name="sums")
-            d_rows[r] = dpool.tile([P, N], BF16, name="d_rows")
+            first, size = group_of[r]
+            if r == first:
+                d_tiles[first] = dpool.tile([P, size, N], BF16, name="d_sb")
+                sums[first] = small.tile([P, size], F32, name="sums")
+            rows = w_tiles[r - r % LOAD_TILES][:, r % LOAD_TILES, :]
             nc.vector.scalar_tensor_tensor(
-                out=d_rows[r][:],
-                in0=w_rows[r][:],
+                out=d_tiles[first][:, r - first, :],
+                in0=rows,
                 scalar=THRESHOLD,
-                in1=w_rows[r][:],
+                in1=rows,
                 op0=ALU.is_gt,
                 op1=ALU.mult,
-                accum_out=sums[r // 2][:, r % 2 : r % 2 + 1],
+                accum_out=sums[first][:, r - first : r - first + 1],
             )
 
-        def invert_sums(i):
-            scales_of_rows[i] = small.tile([P, 2], F32, name="scales_of_rows")
-            nc.vector.reciprocal(scales_of_rows[i][:], sums[i][:])
+        def invert_sums(first, size):
+            inverses[first] = small.tile([P, size], F32, name="rinv")
+            nc.vector.reciprocal(inverses[first][:], sums[first][:])
 
         def normalise(r):
-            rows = d_rows[r][:]
-            scale = scales_of_rows[r // 2][:, r % 2 : r % 2 + 1]
+            first = group_of[r][0]
+            rows = d_tiles[first][:, r - first, :]
+            inverse = inverses[first][:, r - first : r - first + 1]
             if normalised_on_scalar(r):
-                nc.scalar.activation(out=rows, in_=rows, func=ACT.Copy, scale=scale)
+                nc.scalar.activation(out=rows, in_=rows, func=ACT.Copy, scale=inverse)
             else:
-                nc.vector.tensor_scalar_mul(out=rows, in0=rows, scalar1=scale)
+                nc.vector.tensor_scalar_mul(out=rows, in0=rows, scalar1=inverse)
 
         def transpose_rows(r):
+            first = group_of[r][0]
             bank = tpsum.tile([P, PASSES * PACK, P], BF16, name="bank")
             for k in range(PASSES * PACK):
-                first = 2 * P * (k // 2) + k % 2
-                nc.tensor.transpose(bank[:, k, :], d_rows[r][:, first : first + 2 * P - 1 : 2], ident[:])
+                column = 2 * P * (k // 2) + k % 2
+                nc.tensor.transpose(
+                    bank[:, k, :], d_tiles[first][:, r - first, column : column + 2 * P - 1 : 2], ident[:]
+                )
             banks[r] = bank
 
         def regroup(r):
-            if r % 2 == 0:
-                grouped[r // 2] = gpool.tile([P, PASSES, PAIR_COLS, PACK], BF16, name="grouped", align_bytes=64)
-            dst = grouped[r // 2][:, :, (r % 2) * P : (r % 2 + 1) * P, :]
+            first, size = group_of[r]
+            if r == first:
+                grouped[first] = gpool.tile([P, PASSES, size * P, PACK], BF16, name="grouped", align_bytes=64)
+            dst = grouped[first][:, :, (r - first) * P : (r - first + 1) * P, :]
             src = banks[r][:].rearrange("p (c t) m -> p c m t", t=PACK)
             if regrouped_on_vector(r):
                 nc.vector.tensor_copy(out=dst, in_=src)
             else:
                 nc.scalar.copy(out=dst, in_=src)
 
-        def quantise(i):
-            codes = qpool.tile([P, PASSES * PAIR_COLS], U32, name="codes", align_bytes=64)
-            scales = qpool.tile([P, PASSES * PAIR_COLS], U8, name="scales", align_bytes=64)
+        def quantise(first, size):
+            codes = qpool.tile([P, PASSES * size * P], U32, name="codes", align_bytes=64)
+            scales = qpool.tile([P, PASSES * size * P], U8, name="scales", align_bytes=64)
             nc.vector.quantize_mx(
                 out=codes[:].bitcast(FP8X4),
                 scales=scales[:],
-                in_=grouped[i][:].rearrange("p c m t -> p (c m t)"),
+                in_=grouped[first][:].rearrange("p c m t -> p (c m t)"),
             )
-            quantised[i] = (codes, scales)
+            quantised[first] = (codes, scales)
 
-        def multiply(i):
-            b = i // PAIRS_PER_BATCH
-            codes, scales = quantised[i]
-            products[i] = apsum.tile([P, PAIR_COLS], F32, name="products")
+        def multiply(first, size):
+            b = first // TILES_PER_BATCH
+            codes, scales = quantised[first]
+            products[first] = apsum.tile([P, size * P], F32, name="acc")
             for c in range(PASSES):
-                cols = slice(c * PAIR_COLS, (c + 1) * PAIR_COLS)
+                cols = slice(c * size * P, (c + 1) * size * P)
                 nc.tensor.matmul_mx(
-                    out=products[i][:],
+                    out=products[first][:],
                     lhsT=seg_codes[:, b, c, :].bitcast(FP8X4),
                     lhsT_scale=seg_scales[:, b, c, :],
                     rhs=codes[:, cols].bitcast(FP8X4),
@@ -179,43 +215,50 @@ def tile_regu_diff_t_kernel(tc, seg, W, out):
                     stop=(c == PASSES - 1),
                 )
 
-        def leave_psum(i):
-            results[i] = opool.tile([P, PAIR_COLS], F32, name="results")
-            nc.scalar.copy(out=results[i][:], in_=products[i][:])
+        def leave_psum(first, size):
+            results[first] = opool.tile([P, size * P], F32, name="o_sb")
+            nc.scalar.copy(out=results[first][:], in_=products[first][:])
 
-        def store(i):
-            first = (i % PAIRS_PER_BATCH) * PAIR_COLS
-            nc.sync.dma_start(out=out_v[i // PAIRS_PER_BATCH][:, first : first + PAIR_COLS], in_=results[i][:])
+        def store(first, size):
+            column = (first % TILES_PER_BATCH) * P
+            nc.sync.dma_start(
+                out=out_v[first // TILES_PER_BATCH][:, column : column + size * P], in_=results[first][:]
+            )
 
         with tc.manual_schedule():
             for b in range(BATCH):
-                load_rows(b)
+                load_rows(b, 1)
                 load_seg(b)
-            for r in range(BATCH, AHEAD):
-                load_rows(r)
+            for r in range(BATCH, LOADS_AHEAD * LOAD_TILES, LOAD_TILES):
+                load_rows(r, LOAD_TILES)
 
-            for s in range(STEPS):
+            for s in range(steps):
+                refill = s + (LOADS_AHEAD - 1) * LOAD_TILES
+                if s > 0 and s % LOAD_TILES == 0 and refill < ROW_TILES:
+                    load_rows(refill, LOAD_TILES)
                 if s < ROW_TILES:
                     threshold_and_sum(s)
-                if s + AHEAD < ROW_TILES:
-                    load_rows(s + AHEAD)
-                if s % 2 == 0 and 0 <= s // 2 - 1 < PAIRS:
-                    invert_sums(s // 2 - 1)
+                for first, size in groups:
+                    if s == invert_step(first, size):
+                        invert_sums(first, size)
                 if 0 <= s - 3 < BATCH:
                     quantise_seg(s - 3)
-                if 0 <= s - NORMALISE_AFTER < ROW_TILES:
-                    normalise(s - NORMALISE_AFTER)
                 if s < BATCH:
                     transpose_seg(s)
-                if 0 <= s - NORMALISE_AFTER < ROW_TILES:
-                    transpose_rows(s - NORMALISE_AFTER)
+                for r in range(ROW_TILES):
+                    if s == normalise_step(*group_of[r], r):
+                        normalise(r)
+                        transpose_rows(r)
                 if 0 <= s - 1 < BATCH:
                     regroup_seg(s - 1)
-                if 0 <= s - REGROUP_AFTER < ROW_TILES:
-                    regroup(s - REGROUP_AFTER)
-                if (s - QUANTISE_AFTER) % 2 == 0 and 0 <= (s - QUANTISE_AFTER) // 2 < PAIRS:
-                    quantise((s - QUANTISE_AFTER) // 2)
-                    multiply((s - QUANTISE_AFTER) // 2)
-                if (s - LEAVE_AFTER) % 2 == 0 and 0 <= (s - LEAVE_AFTER) // 2 < PAIRS:
-                    leave_psum((s - LEAVE_AFTER) // 2)
-                    store((s - LEAVE_AFTER) // 2)
+                for r in range(ROW_TILES):
+                    if s == normalise_step(*group_of[r], r) + REGROUP_LAG:
+                        regroup(r)
+                for first, size in groups:
+                    if s == quantise_step(first, size):
+                        quantise(first, size)
+                        multiply(first, size)
+                for first, size in groups:
+                    if s == quantise_step(first, size) + LEAVE_LAG:
+                        leave_psum(first, size)
+                        store(first, size)

from contextlib import ExitStack

import concourse.mybir as mybir
from concourse.masks import make_identity

BF16 = mybir.dt.bfloat16
F32 = mybir.dt.float32
U32 = mybir.dt.uint32
U8 = mybir.dt.uint8
FP8X4 = mybir.dt.float8_e4m3fn_x4
ALU = mybir.AluOpType
ACT = mybir.ActivationFunctionType

BATCH = 8
CHANNELS = 128
N = 1024
P = 128
THRESHOLD = 0.85
FLOPS = 2 * BATCH * CHANNELS * N * N

PASSES = 2
PACK = 4
ROW_TILES = BATCH * N // P
TILES_PER_BATCH = N // P
LOAD_TILES = 4
LOADS_AHEAD = 6

GROUP_SIZES = [4] * 14 + [2] * 4

REGROUP_LAG = 2
QUANTISE_LAG = 3
LEAVE_LAG = 1


def make_groups():
    groups = []
    for size in GROUP_SIZES:
        groups.append((sum(GROUP_SIZES[: len(groups)]), size))
    return groups


def invert_step(first, size):
    return first + size


def normalise_step(first, size, r):
    return invert_step(first, size) + 1 + (r - first)


def quantise_step(first, size):
    return normalise_step(first, size, first + size - 1) + REGROUP_LAG + QUANTISE_LAG


def normalised_on_scalar(r):
    return r % 8 in (1, 3, 7) and r < ROW_TILES - 2 * TILES_PER_BATCH


def regrouped_on_vector(r):
    return r == ROW_TILES - 2


def tile_regu_diff_t_kernel(tc, seg, W, out):
    nc = tc.nc
    seg_v = seg.rearrange("b d r c -> b d (r c)")
    w_v = W.rearrange("b (j p) n -> b p j n", p=P)
    out_v = out.rearrange("b d r c -> b d (r c)")
    groups = make_groups()
    group_of = {}
    for first, size in groups:
        for r in range(first, first + size):
            group_of[r] = (first, size)
    steps = quantise_step(*groups[-1]) + LEAVE_LAG + 1

    with ExitStack() as ctx:
        const = ctx.enter_context(tc.tile_pool(name="const", bufs=1))
        wpool = ctx.enter_context(tc.tile_pool(name="wpool", bufs=LOADS_AHEAD))
        dpool = ctx.enter_context(tc.tile_pool(name="dpool", bufs=4))
        small = ctx.enter_context(tc.tile_pool(name="small", bufs=6))
        gpool = ctx.enter_context(tc.tile_pool(name="gpool", bufs=5))
        qpool = ctx.enter_context(tc.tile_pool(name="qpool", bufs=3))
        opool = ctx.enter_context(tc.tile_pool(name="opool", bufs=3))
        tpsum = ctx.enter_context(tc.psum_pool(name="tpsum", bufs=6))
        apsum = ctx.enter_context(tc.psum_pool(name="apsum", bufs=2))

        ident = const.tile([P, P], BF16)
        make_identity(nc, ident[:])
        ident_f32 = const.tile([P, P], F32)
        make_identity(nc, ident_f32[:])

        seg_sb = const.tile([P, BATCH, N], BF16)
        seg_grouped = const.tile([P, BATCH, PASSES, CHANNELS, PACK], BF16, align_bytes=64)
        seg_codes = const.tile([P, BATCH, PASSES, CHANNELS], U32, align_bytes=64)
        seg_scales = const.tile([P, BATCH, PASSES, CHANNELS], U8, align_bytes=64)

        w_tiles = {}
        banks = {}
        seg_banks = {}
        d_tiles = {}
        sums = {}
        inverses = {}
        grouped = {}
        quantised = {}
        products = {}
        results = {}

        def load_rows(r, count):
            base = r - r % LOAD_TILES
            if r == base:
                w_tiles[base] = wpool.tile([P, LOAD_TILES, N], BF16, name="w_sb")
            j = r % TILES_PER_BATCH
            nc.sync.dma_start(
                out=w_tiles[base][:, r - base : r - base + count, :],
                in_=w_v[r // TILES_PER_BATCH][:, j : j + count, :],
            )

        def load_seg(b):
            nc.sync.dma_start(out=seg_sb[:, b, :], in_=seg_v[b])

        def transpose_seg(b):
            words = seg_sb[:, b, :].bitcast(F32)
            bank = tpsum.tile([P, PASSES * 2, CHANNELS], F32, name="bank")
            for k in range(PASSES * 2):
                nc.tensor.transpose(bank[:, k, :], words[:, k * P : (k + 1) * P], ident_f32[:])
            seg_banks[b] = bank

        def regroup_seg(b):
            nc.scalar.copy(
                out=seg_grouped[:, b]
                .rearrange("p c d t -> p c (d t)")
                .bitcast(F32)
                .rearrange("p c (d u) -> p c d u", u=2),
                in_=seg_banks[b][:].rearrange("p (c u) d -> p c d u", u=2),
            )

        def quantise_seg(b):
            nc.vector.quantize_mx(
                out=seg_codes[:, b].rearrange("p c d -> p (c d)").bitcast(FP8X4),
                scales=seg_scales[:, b].rearrange("p c d -> p (c d)"),
                in_=seg_grouped[:, b].rearrange("p c d t -> p (c d t)"),
            )

        def threshold_and_sum(r):
            first, size = group_of[r]
            if r == first:
                d_tiles[first] = dpool.tile([P, size, N], BF16, name="d_sb")
                sums[first] = small.tile([P, size], F32, name="sums")
            rows = w_tiles[r - r % LOAD_TILES][:, r % LOAD_TILES, :]
            nc.vector.scalar_tensor_tensor(
                out=d_tiles[first][:, r - first, :],
                in0=rows,
                scalar=THRESHOLD,
                in1=rows,
                op0=ALU.is_gt,
                op1=ALU.mult,
                accum_out=sums[first][:, r - first : r - first + 1],
            )

        def invert_sums(first, size):
            inverses[first] = small.tile([P, size], F32, name="rinv")
            nc.vector.reciprocal(inverses[first][:], sums[first][:])

        def normalise(r):
            first = group_of[r][0]
            rows = d_tiles[first][:, r - first, :]
            inverse = inverses[first][:, r - first : r - first + 1]
            if normalised_on_scalar(r):
                nc.scalar.activation(out=rows, in_=rows, func=ACT.Copy, scale=inverse)
            else:
                nc.vector.tensor_scalar_mul(out=rows, in0=rows, scalar1=inverse)

        def transpose_rows(r):
            first = group_of[r][0]
            bank = tpsum.tile([P, PASSES * PACK, P], BF16, name="bank")
            for k in range(PASSES * PACK):
                column = 2 * P * (k // 2) + k % 2
                nc.tensor.transpose(
                    bank[:, k, :], d_tiles[first][:, r - first, column : column + 2 * P - 1 : 2], ident[:]
                )
            banks[r] = bank

        def regroup(r):
            first, size = group_of[r]
            if r == first:
                grouped[first] = gpool.tile([P, PASSES, size * P, PACK], BF16, name="grouped", align_bytes=64)
            dst = grouped[first][:, :, (r - first) * P : (r - first + 1) * P, :]
            src = banks[r][:].rearrange("p (c t) m -> p c m t", t=PACK)
            if regrouped_on_vector(r):
                nc.vector.tensor_copy(out=dst, in_=src)
            else:
                nc.scalar.copy(out=dst, in_=src)

        def quantise(first, size):
            codes = qpool.tile([P, PASSES * size * P], U32, name="codes", align_bytes=64)
            scales = qpool.tile([P, PASSES * size * P], U8, name="scales", align_bytes=64)
            nc.vector.quantize_mx(
                out=codes[:].bitcast(FP8X4),
                scales=scales[:],
                in_=grouped[first][:].rearrange("p c m t -> p (c m t)"),
            )
            quantised[first] = (codes, scales)

        def multiply(first, size):
            b = first // TILES_PER_BATCH
            codes, scales = quantised[first]
            products[first] = apsum.tile([P, size * P], F32, name="acc")
            for c in range(PASSES):
                cols = slice(c * size * P, (c + 1) * size * P)
                nc.tensor.matmul_mx(
                    out=products[first][:],
                    lhsT=seg_codes[:, b, c, :].bitcast(FP8X4),
                    lhsT_scale=seg_scales[:, b, c, :],
                    rhs=codes[:, cols].bitcast(FP8X4),
                    rhs_scale=scales[:, cols],
                    start=(c == 0),
                    stop=(c == PASSES - 1),
                )

        def leave_psum(first, size):
            results[first] = opool.tile([P, size * P], F32, name="o_sb")
            nc.scalar.copy(out=results[first][:], in_=products[first][:])

        def store(first, size):
            column = (first % TILES_PER_BATCH) * P
            nc.sync.dma_start(
                out=out_v[first // TILES_PER_BATCH][:, column : column + size * P], in_=results[first][:]
            )

        with tc.manual_schedule():
            for b in range(BATCH):
                load_rows(b, 1)
                load_seg(b)
            for r in range(BATCH, LOADS_AHEAD * LOAD_TILES, LOAD_TILES):
                load_rows(r, LOAD_TILES)

            for s in range(steps):
                refill = s + (LOADS_AHEAD - 1) * LOAD_TILES
                if s > 0 and s % LOAD_TILES == 0 and refill < ROW_TILES:
                    load_rows(refill, LOAD_TILES)
                if s < ROW_TILES:
                    threshold_and_sum(s)
                for first, size in groups:
                    if s == invert_step(first, size):
                        invert_sums(first, size)
                if 0 <= s - 3 < BATCH:
                    quantise_seg(s - 3)
                if s < BATCH:
                    transpose_seg(s)
                for r in range(ROW_TILES):
                    if s == normalise_step(*group_of[r], r):
                        normalise(r)
                        transpose_rows(r)
                if 0 <= s - 1 < BATCH:
                    regroup_seg(s - 1)
                for r in range(ROW_TILES):
                    if s == normalise_step(*group_of[r], r) + REGROUP_LAG:
                        regroup(r)
                for first, size in groups:
                    if s == quantise_step(first, size):
                        quantise(first, size)
                        multiply(first, size)
                for first, size in groups:
                    if s == quantise_step(first, size) + LEAVE_LAG:
                        leave_psum(first, size)
                        store(first, size)
